import numpy as np
import ml_dtypes


def mxq(x, axis, fmt="e4m3"):
    dtype, down = {"e4m3": (ml_dtypes.float8_e4m3fn, 7), "e5m2": (ml_dtypes.float8_e5m2, 14)}[fmt]
    v = np.moveaxis(np.asarray(x, np.float32).astype(ml_dtypes.bfloat16).astype(np.float64), axis, -1)
    blocks = v.reshape(v.shape[:-1] + (-1, 32))
    amax = np.abs(blocks).max(-1, keepdims=True)
    byte = np.maximum(np.where(amax > 0, np.frexp(amax)[1] - 1 + 127, 0) - down, 1)
    scale = np.exp2(byte - 127.0)
    codes = (blocks / scale).astype(np.float32).astype(dtype).astype(np.float64)
    return np.moveaxis((codes * scale).reshape(v.shape), -1, axis)


WIDE = False


def mx_kscale(k):
    if not WIDE:
        return np.ones(k)
    levels = np.array([10, -10, 5, -5, 0])
    if k % 512:
        return np.exp2(np.random.permutation(np.resize(levels, k // 32))).repeat(32)
    a = np.empty((k // 512, 16))
    for p in range(k // 512):
        a[p, :8] = np.random.permutation(np.resize(levels, 8))
        for g in range(8):
            far = levels[np.abs(levels - a[p, g]) >= 10]
            a[p, g + 8] = far[np.random.randint(len(far))]
    return np.exp2(a.ravel()).repeat(32)


BF16 = ml_dtypes.bfloat16


def bf(x):
    return np.asarray(x, np.float32).astype(BF16)


def f64(x):
    return np.asarray(x).astype(np.float64)


B, T, HID, H, D, QB = 1, 1024, 1536, 12, 128, 512
LN_EPS = 1e-5


def layer_norm(u):
    mu = u.mean(-1, keepdims=True)
    var = ((u - mu) ** 2).mean(-1, keepdims=True)
    return (u - mu) * (1.0 / np.sqrt(var + LN_EPS))


def feature_map(u, gamma, beta):
    return layer_norm(u * gamma + beta)


def setup_inputs():
    s = mx_kscale(HID)
    return {"hidden_states": bf(np.random.standard_normal((B, T, HID)) * s),
            "Wq": bf(np.random.standard_normal((H * D, HID)) / np.sqrt(HID) / s),
            "Wk": bf(np.random.standard_normal((H * D, HID)) / np.sqrt(HID) / s),
            "gamma": bf(1.0 + 0.1 * np.random.standard_normal(D)),
            "beta": bf(0.1 * np.random.standard_normal(D))}


def reference(hidden_states, Wq, Wk, gamma, beta):
    g, b = f64(gamma), f64(beta)
    xq = mxq(f64(hidden_states), 2, "e4m3")
    q = (xq @ mxq(f64(Wq), 1, "e4m3").T).reshape(B, T, H, D)
    k = (xq @ mxq(f64(Wk), 1, "e4m3").T).reshape(B, T, H, D)
    q_feat = feature_map(q, g, b) * (D ** -0.5)
    k_feat = feature_map(k, g, b)
    return q_feat, k_feat

@@ -1,0 +1,414 @@
+from contextlib import ExitStack
+
+import concourse.mybir as mybir
+from concourse.masks import make_identity
+
+F32 = mybir.dt.float32
+BF16 = mybir.dt.bfloat16
+U32 = mybir.dt.uint32
+U8 = mybir.dt.uint8
+FP8X4 = mybir.dt.float8_e4m3fn_x4
+ALU = mybir.AluOpType
+ACT = mybir.ActivationFunctionType
+
+P = 128
+TOKENS = 1024
+K = 1536
+D = 128
+TOKEN_TILES = TOKENS // P
+K_PASS = 4 * P
+PASSES = K // K_PASS
+WORDS_PER_PASS = K_PASS // 2
+LN_EPS = 1e-5
+GROUPS_PER_WEIGHT = 3
+BATCHES = 2 * 2 * GROUPS_PER_WEIGHT
+HEAD_TILES = 16
+
+CHUNKS = [("w", 0), ("x", 0), ("x", 1), ("w", 1), ("x", 2), ("x", 3)] + [("w", n) for n in range(2, 12)]
+FIRST_CHUNKS = 7
+
+FLOPS = 2 * TOKENS * (2 * K) * K
+
+
+def tile_rebasedlinearattention_pa_kernel(tc, hidden_states, Wq, Wk, gamma, beta, out_0, out_1):
+    nc = tc.nc
+    x_view = hidden_states.flatten_outer_dims().rearrange("(p i) k -> p i k", i=TOKEN_TILES)
+    w_views = [w.rearrange("(h p) k -> p h k", p=P) for w in (Wq, Wk)]
+    out_views = [
+        o.rearrange("b t h d -> (b t) (h d)").rearrange("(p i) c -> p i c", i=TOKEN_TILES) for o in (out_0, out_1)
+    ]
+
+    with ExitStack() as ctx:
+        keep = ctx.enter_context(tc.tile_pool(name="keep", bufs=1))
+        w_rows = ctx.enter_context(tc.tile_pool(name="w_rows", bufs=8))
+        grouped_pool = ctx.enter_context(tc.tile_pool(name="grouped", bufs=8))
+        w_mx = ctx.enter_context(tc.tile_pool(name="w_mx", bufs=4))
+        turned_pool = ctx.enter_context(tc.tile_pool(name="turned", bufs=4))
+        result_pool = ctx.enter_context(tc.tile_pool(name="result", bufs=5))
+        small = ctx.enter_context(tc.tile_pool(name="small", bufs=4))
+        psum_in = ctx.enter_context(tc.psum_pool(name="psum_in", bufs=2))
+        psum_acc = ctx.enter_context(tc.psum_pool(name="psum_acc", bufs=2))
+        psum_back = ctx.enter_context(tc.psum_pool(name="psum_back", bufs=4))
+        ctx.enter_context(tc.manual_schedule())
+
+        x_rows = keep.tile([P, TOKEN_TILES, K], BF16)
+        x_codes = keep.tile([P, PASSES, TOKENS], U32, align_bytes=64)
+        x_scales = keep.tile([P, PASSES, TOKENS], U8, align_bytes=64)
+        live = {}
+
+
+        def load(k):
+            kind, n = CHUNKS[k]
+            if kind == "x":
+                nc.sync.dma_start(out=x_rows[:, 2 * n : 2 * n + 2, :], in_=x_view[:, 2 * n : 2 * n + 2, :])
+            else:
+                rows = w_rows.tile([P, 2, K], BF16, tag="rows", name="rows")
+                live[("rows", k)] = rows
+                head = 2 * n % 12
+                nc.sync.dma_start(out=rows[:], in_=w_views[n // 6][:, head : head + 2, :])
+
+        def transpose_in(k, g, pool):
+            kind, n = CHUNKS[k]
+            source = x_rows[:, 2 * n : 2 * n + 2, :] if kind == "x" else live[("rows", k)][:]
+            bank = pool.tile([P, 2, 2, P], F32, tag="bank", name="in_bank")
+            live[("in", k, g)] = bank
+            for row_tile in range(2):
+                words = source[:, row_tile, :].bitcast(F32)
+                for u in range(2):
+                    first = WORDS_PER_PASS * g + u
+                    nc.tensor.transpose(
+                        bank[:, row_tile, u, :], words[:, first : WORDS_PER_PASS * (g + 1) : 2], identity[:]
+                    )
+
+        def regroup(k, g, engine):
+            grouped = grouped_pool.tile([P, 2 * P * 4], BF16, align_bytes=64, tag="grouped", name="grouped")
+            live[("grouped", k, g)] = grouped
+            dst = grouped[:].bitcast(F32).rearrange("p (t r u) -> p t r u", t=2, r=P, u=2)
+            src = live[("in", k, g)][:].rearrange("p t u r -> p t r u")
+            if engine == "vector":
+                nc.vector.tensor_copy(out=dst, in_=src)
+            else:
+                nc.scalar.copy(out=dst, in_=src)
+
+        def quantise(k, g):
+            kind, n = CHUNKS[k]
+            if kind == "x":
+                codes, scales = x_codes, x_scales
+                cols = slice(2 * P * n, 2 * P * (n + 1))
+            else:
+                group = n // 2
+                if ("codes", group) not in live:
+                    shape = [P, PASSES, 4 * D]
+                    live[("codes", group)] = w_mx.tile(shape, U32, align_bytes=64, tag="codes", name="w_codes")
+                    live[("scales", group)] = w_mx.tile(shape, U8, align_bytes=64, tag="scales", name="w_scales")
+                codes, scales = live[("codes", group)], live[("scales", group)]
+                cols = slice(2 * D * (n % 2), 2 * D * (n % 2 + 1))
+            nc.vector.quantize_mx(
+                out=codes[:, g, cols].bitcast(FP8X4), scales=scales[:, g, cols], in_=live[("grouped", k, g)][:]
+            )
+
+        def streamed(k):
+            return FIRST_CHUNKS <= k < len(CHUNKS)
+
+
+        def exists(b):
+            return 0 <= b < BATCHES
+
+        def result_of(b):
+            if ("result", b) not in live:
+                live[("result", b)] = result_pool.tile([P, 4, 4 * D], F32, tag="result", name="result")
+            return live[("result", b)]
+
+        def stats_of(b):
+            if ("stats", b) not in live:
+                live[("stats", b)] = small.tile([P, HEAD_TILES, 6], F32, tag="stats", name="stats")
+            return live[("stats", b)]
+
+        def product(acc, lhs_codes, lhs_scales, lhs_cols, rhs_codes, rhs_scales, rhs_cols):
+            for g in range(PASSES):
+                nc.tensor.matmul_mx(
+                    out=acc,
+                    lhsT=lhs_codes[:, g, lhs_cols].bitcast(FP8X4),
+                    lhsT_scale=lhs_scales[:, g, lhs_cols],
+                    rhs=rhs_codes[:, g, rhs_cols].bitcast(FP8X4),
+                    rhs_scale=rhs_scales[:, g, rhs_cols],
+                    start=(g == 0),
+                    stop=(g == PASSES - 1),
+                )
+
+        def straight_matmuls(b, pair):
+            if not exists(b):
+                return
+            acc = psum_acc.tile([P, 2, 2 * D], F32, tag="bank", name="straight_acc")
+            live[("straight", b, pair)] = acc
+            for t in range(2):
+                i = 4 * (b % 2) + 2 * pair + t
+                product(
+                    acc[:, t, :], x_codes, x_scales, slice(P * i, P * (i + 1)),
+                    live[("codes", b // 2)], live[("scales", b // 2)], slice(0, 2 * D),
+                )
+
+        def straight_view(b, pair):
+            return result_of(b)[:, 2 * pair : 2 * pair + 2, 0 : 2 * D].rearrange("p t (h d) -> p t h d", d=D)
+
+        def times_gamma(b, pair):
+            if not exists(b):
+                return
+            nc.vector.tensor_tensor(
+                out=straight_view(b, pair),
+                in0=live[("straight", b, pair)][:].rearrange("p t (h d) -> p t h d", d=D),
+                in1=affine_rows[:, 0:D].unsqueeze(1).unsqueeze(1).to_broadcast([P, 2, 2, D]),
+                op=ALU.mult,
+            )
+
+        def plus_beta(b, pair):
+            if not exists(b):
+                return
+            nc.gpsimd.tensor_tensor(
+                out=straight_view(b, pair),
+                in0=straight_view(b, pair),
+                in1=affine_rows[:, D : 2 * D].unsqueeze(1).unsqueeze(1).to_broadcast([P, 2, 2, D]),
+                op=ALU.add,
+            )
+
+        def straight_stats(b, pair):
+            if not exists(b):
+                return
+            for t in range(2):
+                for h in range(2):
+                    nc.vector.bn_stats(
+                        out=stats_of(b)[:, 4 * pair + 2 * t + h, :],
+                        in_=result_of(b)[:, 2 * pair + t, D * h : D * (h + 1)],
+                    )
+
+        def turned_matmuls(b, head):
+            if not exists(b):
+                return
+            acc = psum_acc.tile([P, 4 * P], F32, tag="bank", name="turned_acc")
+            live[("turned_acc", b, head)] = acc
+            product(
+                acc[:], live[("codes", b // 2)], live[("scales", b // 2)], slice(D * (2 + head), D * (3 + head)),
+                x_codes, x_scales, slice(4 * P * (b % 2), 4 * P * (b % 2 + 1)),
+            )
+
+        def turned_affine(b, head):
+            if not exists(b):
+                return
+            turned = turned_pool.tile([P, 4 * P], F32, tag="turned", name="turned")
+            live[("turned", b, head)] = turned
+            nc.scalar.activation(
+                out=turned[:],
+                in_=live[("turned_acc", b, head)][:],
+                func=ACT.Identity,
+                scale=affine_cols[:, 0:1],
+                bias=affine_cols[:, 1:2],
+            )
+
+        def turn_back(b, head):
+            if not exists(b):
+                return
+            bank = psum_back.tile([P, 4, D], F32, tag="bank", name="back")
+            live[("back", b, head)] = bank
+            for t in range(4):
+                nc.tensor.transpose(bank[:, t, :], live[("turned", b, head)][:, P * t : P * (t + 1)], identity[:])
+
+        def turned_stats(b, head):
+            if not exists(b):
+                return
+            for t in range(4):
+                nc.vector.bn_stats(out=stats_of(b)[:, 8 + 4 * head + t, :], in_=live[("back", b, head)][:, t, :])
+
+
+        def pair_sums(b):
+            if not exists(b):
+                return
+            live[("sums", b)] = small.tile([P, HEAD_TILES, 3], F32, tag="sums", name="sums")
+            nc.vector.tensor_reduce(
+                out=live[("sums", b)][:],
+                in_=stats_of(b)[:].rearrange("p n (half entry) -> p n entry half", half=2),
+                axis=mybir.AxisListType.X,
+                op=ALU.add,
+            )
+
+        def mean_gap(b):
+            if not exists(b):
+                return
+            live[("gap", b)] = small.tile([P, HEAD_TILES], F32, tag="gap", name="gap")
+            nc.vector.tensor_tensor(
+                out=live[("gap", b)][:], in0=stats_of(b)[:, :, 1], in1=stats_of(b)[:, :, 4], op=ALU.subtract
+            )
+
+        def gap_squared(b):
+            if not exists(b):
+                return
+            live[("gap2", b)] = small.tile([P, HEAD_TILES], F32, tag="gap2", name="gap2")
+            nc.vector.scalar_tensor_tensor(
+                out=live[("gap2", b)][:],
+                in0=live[("gap", b)][:],
+                scalar=D / 4.0,
+                in1=live[("gap", b)][:],
+                op0=ALU.mult,
+                op1=ALU.mult,
+            )
+
+        def spread(b):
+            if not exists(b):
+                return
+            live[("spread", b)] = small.tile([P, HEAD_TILES], F32, tag="spread", name="spread")
+            nc.vector.scalar_tensor_tensor(
+                out=live[("spread", b)][:],
+                in0=live[("sums", b)][:, :, 2],
+                scalar=D * LN_EPS,
+                in1=live[("gap2", b)][:],
+                op0=ALU.add,
+                op1=ALU.add,
+            )
+
+        def factor(b):
+            if not exists(b):
+                return
+            live[("factor", b)] = small.tile([P, HEAD_TILES], F32, tag="factor", name="factor")
+            nc.scalar.activation(
+                out=live[("factor", b)][:],
+                in_=live[("spread", b)][:],
+                func=ACT.Abs_reciprocal_sqrt,
+                scale=(1.0 if b // 2 < GROUPS_PER_WEIGHT else 1.0 / D),
+            )
+
+        def offset(b):
+            if not exists(b):
+                return
+            live[("offset", b)] = small.tile([P, HEAD_TILES], F32, tag="offset", name="offset")
+            nc.vector.scalar_tensor_tensor(
+                out=live[("offset", b)][:],
+                in0=live[("sums", b)][:, :, 1],
+                scalar=-0.5,
+                in1=live[("factor", b)][:],
+                op0=ALU.mult,
+                op1=ALU.mult,
+            )
+
+        def normalise_straight(b, pair):
+            if not exists(b):
+                return
+            for t in range(2):
+                for h in range(2):
+                    n = 4 * pair + 2 * t + h
+                    piece = result_of(b)[:, 2 * pair + t, D * h : D * (h + 1)]
+                    nc.vector.tensor_scalar(
+                        out=piece,
+                        in0=piece,
+                        scalar1=live[("factor", b)][:, n : n + 1],
+                        scalar2=live[("offset", b)][:, n : n + 1],
+                        op0=ALU.mult,
+                        op1=ALU.add,
+                    )
+
+        def normalise_turned(b, head):
+            if not exists(b):
+                return
+            for t in range(4):
+                n = 8 + 4 * head + t
+                nc.scalar.activation(
+                    out=result_of(b)[:, t, D * (2 + head) : D * (3 + head)],
+                    in_=live[("back", b, head)][:, t, :],
+                    func=ACT.Identity,
+                    scale=live[("factor", b)][:, n : n + 1],
+                    bias=live[("offset", b)][:, n : n + 1],
+                )
+
+        def store(b):
+            if not exists(b):
+                return
+            group, half = b // 2, b % 2
+            cols = slice(4 * D * (group % GROUPS_PER_WEIGHT), 4 * D * (group % GROUPS_PER_WEIGHT + 1))
+            nc.sync.dma_start(
+                out=out_views[group // GROUPS_PER_WEIGHT][:, 4 * half : 4 * half + 4, cols], in_=result_of(b)[:]
+            )
+
+
+        for k in range(len(CHUNKS)):
+            load(k)
+        identity = keep.tile([P, P], F32)
+        make_identity(nc, identity[:])
+        ones = keep.tile([P, P], BF16)
+        nc.vector.memset(ones[:], 1.0)
+        gamma_beta = keep.tile([P, 2 * D], BF16)
+        nc.vector.memset(gamma_beta[:], 0.0)
+        one = keep.tile([P, 1], F32)
+        nc.vector.memset(one[:], 1.0)
+        nc.scalar.dma_start(out=gamma_beta[0:1, 0:D], in_=gamma.unsqueeze(0))
+        nc.scalar.dma_start(out=gamma_beta[0:1, D : 2 * D], in_=beta.unsqueeze(0))
+        nc.scalar.activation(out=one[:], in_=one[:], func=ACT.Abs_reciprocal_sqrt)
+
+        early_pools = [psum_in, psum_back, psum_acc, psum_back]
+        for n in range(FIRST_CHUNKS * PASSES):
+            transpose_in(n // PASSES, n % PASSES, early_pools[n % len(early_pools)])
+            regroup(n // PASSES, n % PASSES, "vector" if n % 2 else "scalar")
+            if n > 0:
+                quantise((n - 1) // PASSES, (n - 1) % PASSES)
+        quantise(FIRST_CHUNKS - 1, PASSES - 1)
+
+        rows_bank = psum_back.tile([P, 2 * D], F32, tag="bank", name="rows_bank")
+        nc.tensor.matmul(out=rows_bank[:], lhsT=ones[:], rhs=gamma_beta[:], start=True, stop=True)
+        affine_rows = keep.tile([P, 2 * D], F32)
+        nc.scalar.copy(out=affine_rows[:], in_=rows_bank[:])
+        cols_bank = psum_back.tile([P, 2, 64], F32, tag="bank", name="cols_bank")
+        for which in range(2):
+            nc.tensor.matmul(
+                out=cols_bank[:, which, :],
+                lhsT=gamma_beta[:, D * which : D * (which + 1)],
+                rhs=ones[:, 0:64],
+                start=True,
+                stop=True,
+            )
+        affine_cols = keep.tile([P, 2], F32)
+        nc.scalar.copy(out=affine_cols[:], in_=cols_bank[:, :, 0])
+
+        for b in range(BATCHES + 3):
+            new, old = b + 7, b + 6
+
+            straight_matmuls(b, 0)
+            turned_matmuls(b - 1, 1)
+            offset(b - 3)
+            if streamed(old):
+                quantise(old, 0)
+            turned_affine(b - 1, 0)
+            if streamed(old):
+                regroup(old, 1, "scalar")
+                regroup(old, 2, "scalar")
+            if streamed(new):
+                transpose_in(new, 0, psum_in)
+            turn_back(b - 1, 0)
+            normalise_turned(b - 3, 0)
+            straight_stats(b - 1, 0)
+            turned_stats(b - 2, 1)
+            times_gamma(b, 0)
+            plus_beta(b, 0)
+            pair_sums(b - 2)
+            mean_gap(b - 2)
+            normalise_straight(b - 3, 0)
+            if streamed(old):
+                quantise(old, 2)
+            gap_squared(b - 2)
+
+            straight_matmuls(b, 1)
+            turned_matmuls(b, 0)
+            if streamed(old):
+                quantise(old, 1)
+            normalise_straight(b - 3, 1)
+            spread(b - 2)
+            turned_affine(b - 1, 1)
+            if streamed(new):
+                transpose_in(new, 1, psum_in)
+            turn_back(b - 1, 1)
+            if streamed(new):
+                transpose_in(new, 2, psum_in)
+                regroup(new, 0, "scalar")
+            normalise_turned(b - 3, 1)
+            store(b - 3)
+            factor(b - 2)
+            straight_stats(b - 1, 1)
+            turned_stats(b - 1, 0)
+            times_gamma(b, 1)
+            plus_beta(b, 1)

@@ -184,7 +184,8 @@ def tile_rebasedlinearattention_pa_kernel(tc, hidden_states, Wq, Wk, gamma, beta
         def turned_matmuls(b, head):
             if not exists(b):
                 return
-            acc = psum_acc.tile([P, 4 * P], F32, tag="bank", name="turned_acc")
+            pool = psum_back if (b, head) == (0, 0) else psum_acc
+            acc = pool.tile([P, 4 * P], F32, tag="bank", name="turned_acc")
             live[("turned_acc", b, head)] = acc
             product(
                 acc[:], live[("codes", b // 2)], live[("scales", b // 2)], slice(D * (2 + head), D * (3 + head)),

from contextlib import ExitStack

import concourse.mybir as mybir
from concourse.masks import make_identity

F32 = mybir.dt.float32
BF16 = mybir.dt.bfloat16
U32 = mybir.dt.uint32
U8 = mybir.dt.uint8
FP8X4 = mybir.dt.float8_e4m3fn_x4
ALU = mybir.AluOpType
ACT = mybir.ActivationFunctionType

P = 128
TOKENS = 1024
K = 1536
D = 128
TOKEN_TILES = TOKENS // P
K_PASS = 4 * P
PASSES = K // K_PASS
WORDS_PER_PASS = K_PASS // 2
LN_EPS = 1e-5
GROUPS_PER_WEIGHT = 3
BATCHES = 2 * 2 * GROUPS_PER_WEIGHT
HEAD_TILES = 16

CHUNKS = [("w", 0), ("x", 0), ("x", 1), ("w", 1), ("x", 2), ("x", 3)] + [("w", n) for n in range(2, 12)]
FIRST_CHUNKS = 7

FLOPS = 2 * TOKENS * (2 * K) * K


def tile_rebasedlinearattention_pa_kernel(tc, hidden_states, Wq, Wk, gamma, beta, out_0, out_1):
    nc = tc.nc
    x_view = hidden_states.flatten_outer_dims().rearrange("(p i) k -> p i k", i=TOKEN_TILES)
    w_views = [w.rearrange("(h p) k -> p h k", p=P) for w in (Wq, Wk)]
    out_views = [
        o.rearrange("b t h d -> (b t) (h d)").rearrange("(p i) c -> p i c", i=TOKEN_TILES) for o in (out_0, out_1)
    ]

    with ExitStack() as ctx:
        keep = ctx.enter_context(tc.tile_pool(name="keep", bufs=1))
        w_rows = ctx.enter_context(tc.tile_pool(name="w_rows", bufs=8))
        grouped_pool = ctx.enter_context(tc.tile_pool(name="grouped", bufs=8))
        w_mx = ctx.enter_context(tc.tile_pool(name="w_mx", bufs=4))
        turned_pool = ctx.enter_context(tc.tile_pool(name="turned", bufs=4))
        result_pool = ctx.enter_context(tc.tile_pool(name="result", bufs=5))
        small = ctx.enter_context(tc.tile_pool(name="small", bufs=4))
        psum_in = ctx.enter_context(tc.psum_pool(name="psum_in", bufs=2))
        psum_acc = ctx.enter_context(tc.psum_pool(name="psum_acc", bufs=2))
        psum_back = ctx.enter_context(tc.psum_pool(name="psum_back", bufs=4))
        ctx.enter_context(tc.manual_schedule())

        x_rows = keep.tile([P, TOKEN_TILES, K], BF16)
        x_codes = keep.tile([P, PASSES, TOKENS], U32, align_bytes=64)
        x_scales = keep.tile([P, PASSES, TOKENS], U8, align_bytes=64)
        live = {}


        def load(k):
            kind, n = CHUNKS[k]
            if kind == "x":
                nc.sync.dma_start(out=x_rows[:, 2 * n : 2 * n + 2, :], in_=x_view[:, 2 * n : 2 * n + 2, :])
            else:
                rows = w_rows.tile([P, 2, K], BF16, tag="rows", name="rows")
                live[("rows", k)] = rows
                head = 2 * n % 12
                nc.sync.dma_start(out=rows[:], in_=w_views[n // 6][:, head : head + 2, :])

        def transpose_in(k, g, pool):
            kind, n = CHUNKS[k]
            source = x_rows[:, 2 * n : 2 * n + 2, :] if kind == "x" else live[("rows", k)][:]
            bank = pool.tile([P, 2, 2, P], F32, tag="bank", name="in_bank")
            live[("in", k, g)] = bank
            for row_tile in range(2):
                words = source[:, row_tile, :].bitcast(F32)
                for u in range(2):
                    first = WORDS_PER_PASS * g + u
                    nc.tensor.transpose(
                        bank[:, row_tile, u, :], words[:, first : WORDS_PER_PASS * (g + 1) : 2], identity[:]
                    )

        def regroup(k, g, engine):
            grouped = grouped_pool.tile([P, 2 * P * 4], BF16, align_bytes=64, tag="grouped", name="grouped")
            live[("grouped", k, g)] = grouped
            dst = grouped[:].bitcast(F32).rearrange("p (t r u) -> p t r u", t=2, r=P, u=2)
            src = live[("in", k, g)][:].rearrange("p t u r -> p t r u")
            if engine == "vector":
                nc.vector.tensor_copy(out=dst, in_=src)
            else:
                nc.scalar.copy(out=dst, in_=src)

        def quantise(k, g):
            kind, n = CHUNKS[k]
            if kind == "x":
                codes, scales = x_codes, x_scales
                cols = slice(2 * P * n, 2 * P * (n + 1))
            else:
                group = n // 2
                if ("codes", group) not in live:
                    shape = [P, PASSES, 4 * D]
                    live[("codes", group)] = w_mx.tile(shape, U32, align_bytes=64, tag="codes", name="w_codes")
                    live[("scales", group)] = w_mx.tile(shape, U8, align_bytes=64, tag="scales", name="w_scales")
                codes, scales = live[("codes", group)], live[("scales", group)]
                cols = slice(2 * D * (n % 2), 2 * D * (n % 2 + 1))
            nc.vector.quantize_mx(
                out=codes[:, g, cols].bitcast(FP8X4), scales=scales[:, g, cols], in_=live[("grouped", k, g)][:]
            )

        def streamed(k):
            return FIRST_CHUNKS <= k < len(CHUNKS)


        def exists(b):
            return 0 <= b < BATCHES

        def result_of(b):
            if ("result", b) not in live:
                live[("result", b)] = result_pool.tile([P, 4, 4 * D], F32, tag="result", name="result")
            return live[("result", b)]

        def stats_of(b):
            if ("stats", b) not in live:
                live[("stats", b)] = small.tile([P, HEAD_TILES, 6], F32, tag="stats", name="stats")
            return live[("stats", b)]

        def product(acc, lhs_codes, lhs_scales, lhs_cols, rhs_codes, rhs_scales, rhs_cols):
            for g in range(PASSES):
                nc.tensor.matmul_mx(
                    out=acc,
                    lhsT=lhs_codes[:, g, lhs_cols].bitcast(FP8X4),
                    lhsT_scale=lhs_scales[:, g, lhs_cols],
                    rhs=rhs_codes[:, g, rhs_cols].bitcast(FP8X4),
                    rhs_scale=rhs_scales[:, g, rhs_cols],
                    start=(g == 0),
                    stop=(g == PASSES - 1),
                )

        def straight_matmuls(b, pair):
            if not exists(b):
                return
            acc = psum_acc.tile([P, 2, 2 * D], F32, tag="bank", name="straight_acc")
            live[("straight", b, pair)] = acc
            for t in range(2):
                i = 4 * (b % 2) + 2 * pair + t
                product(
                    acc[:, t, :], x_codes, x_scales, slice(P * i, P * (i + 1)),
                    live[("codes", b // 2)], live[("scales", b // 2)], slice(0, 2 * D),
                )

        def straight_view(b, pair):
            return result_of(b)[:, 2 * pair : 2 * pair + 2, 0 : 2 * D].rearrange("p t (h d) -> p t h d", d=D)

        def times_gamma(b, pair):
            if not exists(b):
                return
            nc.vector.tensor_tensor(
                out=straight_view(b, pair),
                in0=live[("straight", b, pair)][:].rearrange("p t (h d) -> p t h d", d=D),
                in1=affine_rows[:, 0:D].unsqueeze(1).unsqueeze(1).to_broadcast([P, 2, 2, D]),
                op=ALU.mult,
            )

        def plus_beta(b, pair):
            if not exists(b):
                return
            nc.gpsimd.tensor_tensor(
                out=straight_view(b, pair),
                in0=straight_view(b, pair),
                in1=affine_rows[:, D : 2 * D].unsqueeze(1).unsqueeze(1).to_broadcast([P, 2, 2, D]),
                op=ALU.add,
            )

        def straight_stats(b, pair):
            if not exists(b):
                return
            for t in range(2):
                for h in range(2):
                    nc.vector.bn_stats(
                        out=stats_of(b)[:, 4 * pair + 2 * t + h, :],
                        in_=result_of(b)[:, 2 * pair + t, D * h : D * (h + 1)],
                    )

        def turned_matmuls(b, head):
            if not exists(b):
                return
            pool = psum_back if (b, head) == (0, 0) else psum_acc
            acc = pool.tile([P, 4 * P], F32, tag="bank", name="turned_acc")
            live[("turned_acc", b, head)] = acc
            product(
                acc[:], live[("codes", b // 2)], live[("scales", b // 2)], slice(D * (2 + head), D * (3 + head)),
                x_codes, x_scales, slice(4 * P * (b % 2), 4 * P * (b % 2 + 1)),
            )

        def turned_affine(b, head):
            if not exists(b):
                return
            turned = turned_pool.tile([P, 4 * P], F32, tag="turned", name="turned")
            live[("turned", b, head)] = turned
            nc.scalar.activation(
                out=turned[:],
                in_=live[("turned_acc", b, head)][:],
                func=ACT.Identity,
                scale=affine_cols[:, 0:1],
                bias=affine_cols[:, 1:2],
            )

        def turn_back(b, head):
            if not exists(b):
                return
            bank = psum_back.tile([P, 4, D], F32, tag="bank", name="back")
            live[("back", b, head)] = bank
            for t in range(4):
                nc.tensor.transpose(bank[:, t, :], live[("turned", b, head)][:, P * t : P * (t + 1)], identity[:])

        def turned_stats(b, head):
            if not exists(b):
                return
            for t in range(4):
                nc.vector.bn_stats(out=stats_of(b)[:, 8 + 4 * head + t, :], in_=live[("back", b, head)][:, t, :])


        def pair_sums(b):
            if not exists(b):
                return
            live[("sums", b)] = small.tile([P, HEAD_TILES, 3], F32, tag="sums", name="sums")
            nc.vector.tensor_reduce(
                out=live[("sums", b)][:],
                in_=stats_of(b)[:].rearrange("p n (half entry) -> p n entry half", half=2),
                axis=mybir.AxisListType.X,
                op=ALU.add,
            )

        def mean_gap(b):
            if not exists(b):
                return
            live[("gap", b)] = small.tile([P, HEAD_TILES], F32, tag="gap", name="gap")
            nc.vector.tensor_tensor(
                out=live[("gap", b)][:], in0=stats_of(b)[:, :, 1], in1=stats_of(b)[:, :, 4], op=ALU.subtract
            )

        def gap_squared(b):
            if not exists(b):
                return
            live[("gap2", b)] = small.tile([P, HEAD_TILES], F32, tag="gap2", name="gap2")
            nc.vector.scalar_tensor_tensor(
                out=live[("gap2", b)][:],
                in0=live[("gap", b)][:],
                scalar=D / 4.0,
                in1=live[("gap", b)][:],
                op0=ALU.mult,
                op1=ALU.mult,
            )

        def spread(b):
            if not exists(b):
                return
            live[("spread", b)] = small.tile([P, HEAD_TILES], F32, tag="spread", name="spread")
            nc.vector.scalar_tensor_tensor(
                out=live[("spread", b)][:],
                in0=live[("sums", b)][:, :, 2],
                scalar=D * LN_EPS,
                in1=live[("gap2", b)][:],
                op0=ALU.add,
                op1=ALU.add,
            )

        def factor(b):
            if not exists(b):
                return
            live[("factor", b)] = small.tile([P, HEAD_TILES], F32, tag="factor", name="factor")
            nc.scalar.activation(
                out=live[("factor", b)][:],
                in_=live[("spread", b)][:],
                func=ACT.Abs_reciprocal_sqrt,
                scale=(1.0 if b // 2 < GROUPS_PER_WEIGHT else 1.0 / D),
            )

        def offset(b):
            if not exists(b):
                return
            live[("offset", b)] = small.tile([P, HEAD_TILES], F32, tag="offset", name="offset")
            nc.vector.scalar_tensor_tensor(
                out=live[("offset", b)][:],
                in0=live[("sums", b)][:, :, 1],
                scalar=-0.5,
                in1=live[("factor", b)][:],
                op0=ALU.mult,
                op1=ALU.mult,
            )

        def normalise_straight(b, pair):
            if not exists(b):
                return
            for t in range(2):
                for h in range(2):
                    n = 4 * pair + 2 * t + h
                    piece = result_of(b)[:, 2 * pair + t, D * h : D * (h + 1)]
                    nc.vector.tensor_scalar(
                        out=piece,
                        in0=piece,
                        scalar1=live[("factor", b)][:, n : n + 1],
                        scalar2=live[("offset", b)][:, n : n + 1],
                        op0=ALU.mult,
                        op1=ALU.add,
                    )

        def normalise_turned(b, head):
            if not exists(b):
                return
            for t in range(4):
                n = 8 + 4 * head + t
                nc.scalar.activation(
                    out=result_of(b)[:, t, D * (2 + head) : D * (3 + head)],
                    in_=live[("back", b, head)][:, t, :],
                    func=ACT.Identity,
                    scale=live[("factor", b)][:, n : n + 1],
                    bias=live[("offset", b)][:, n : n + 1],
                )

        def store(b):
            if not exists(b):
                return
            group, half = b // 2, b % 2
            cols = slice(4 * D * (group % GROUPS_PER_WEIGHT), 4 * D * (group % GROUPS_PER_WEIGHT + 1))
            nc.sync.dma_start(
                out=out_views[group // GROUPS_PER_WEIGHT][:, 4 * half : 4 * half + 4, cols], in_=result_of(b)[:]
            )


        for k in range(len(CHUNKS)):
            load(k)
        identity = keep.tile([P, P], F32)
        make_identity(nc, identity[:])
        ones = keep.tile([P, P], BF16)
        nc.vector.memset(ones[:], 1.0)
        gamma_beta = keep.tile([P, 2 * D], BF16)
        nc.vector.memset(gamma_beta[:], 0.0)
        one = keep.tile([P, 1], F32)
        nc.vector.memset(one[:], 1.0)
        nc.scalar.dma_start(out=gamma_beta[0:1, 0:D], in_=gamma.unsqueeze(0))
        nc.scalar.dma_start(out=gamma_beta[0:1, D : 2 * D], in_=beta.unsqueeze(0))
        nc.scalar.activation(out=one[:], in_=one[:], func=ACT.Abs_reciprocal_sqrt)

        early_pools = [psum_in, psum_back, psum_acc, psum_back]
        for n in range(FIRST_CHUNKS * PASSES):
            transpose_in(n // PASSES, n % PASSES, early_pools[n % len(early_pools)])
            regroup(n // PASSES, n % PASSES, "vector" if n % 2 else "scalar")
            if n > 0:
                quantise((n - 1) // PASSES, (n - 1) % PASSES)
        quantise(FIRST_CHUNKS - 1, PASSES - 1)

        rows_bank = psum_back.tile([P, 2 * D], F32, tag="bank", name="rows_bank")
        nc.tensor.matmul(out=rows_bank[:], lhsT=ones[:], rhs=gamma_beta[:], start=True, stop=True)
        affine_rows = keep.tile([P, 2 * D], F32)
        nc.scalar.copy(out=affine_rows[:], in_=rows_bank[:])
        cols_bank = psum_back.tile([P, 2, 64], F32, tag="bank", name="cols_bank")
        for which in range(2):
            nc.tensor.matmul(
                out=cols_bank[:, which, :],
                lhsT=gamma_beta[:, D * which : D * (which + 1)],
                rhs=ones[:, 0:64],
                start=True,
                stop=True,
            )
        affine_cols = keep.tile([P, 2], F32)
        nc.scalar.copy(out=affine_cols[:], in_=cols_bank[:, :, 0])

        for b in range(BATCHES + 3):
            new, old = b + 7, b + 6

            straight_matmuls(b, 0)
            turned_matmuls(b - 1, 1)
            offset(b - 3)
            if streamed(old):
                quantise(old, 0)
            turned_affine(b - 1, 0)
            if streamed(old):
                regroup(old, 1, "scalar")
                regroup(old, 2, "scalar")
            if streamed(new):
                transpose_in(new, 0, psum_in)
            turn_back(b - 1, 0)
            normalise_turned(b - 3, 0)
            straight_stats(b - 1, 0)
            turned_stats(b - 2, 1)
            times_gamma(b, 0)
            plus_beta(b, 0)
            pair_sums(b - 2)
            mean_gap(b - 2)
            normalise_straight(b - 3, 0)
            if streamed(old):
                quantise(old, 2)
            gap_squared(b - 2)

            straight_matmuls(b, 1)
            turned_matmuls(b, 0)
            if streamed(old):
                quantise(old, 1)
            normalise_straight(b - 3, 1)
            spread(b - 2)
            turned_affine(b - 1, 1)
            if streamed(new):
                transpose_in(new, 1, psum_in)
            turn_back(b - 1, 1)
            if streamed(new):
                transpose_in(new, 2, psum_in)
                regroup(new, 0, "scalar")
            normalise_turned(b - 3, 1)
            store(b - 3)
            factor(b - 2)
            straight_stats(b - 1, 1)
            turned_stats(b - 1, 0)
            times_gamma(b, 1)
            plus_beta(b, 1)
